import numpy as np
import ml_dtypes

BF16 = ml_dtypes.bfloat16


def bf(x):
    return np.asarray(x, np.float32).astype(BF16)


def f32(x):
    return np.asarray(x, np.float32)


def f64(x):
    return np.asarray(x).astype(np.float64)


def striped(idx):
    return np.tile(idx.reshape(-1, 16).T, (8, 1))


D, P, F, S, M, B, A, N = 128, 128, 512, 2048, 256, 8, 64, 512
SLOPE = 0.01


def setup_inputs():
    sc = 1.0 / np.sqrt(F)
    return {
        "table": bf(np.random.standard_normal((D, S))),
        "ment": bf(np.random.standard_normal((D, B))),
        "pw": bf(np.random.standard_normal((P, N))),
        "w_a": bf(sc * np.random.standard_normal((D, M))),
        "w_b": bf(sc * np.random.standard_normal((D, M))),
        "w_c": bf(sc * np.random.standard_normal((D, M))),
        "w_d": bf(sc * np.random.standard_normal((P, M))),
        "b1": f32(0.1 * np.random.standard_normal((M, 1))),
        "offs": striped(np.random.permutation(np.tile(np.arange(S), 2))[:N]),
    }


def reference(table, ment, pw, w_a, w_b, w_c, w_d, b1, offs):
    idx = offs[:16].T.reshape(-1)
    picked = f64(table)[:, idx].reshape(D, B, A)
    u = f64(w_b)[:, None, :] + f64(ment)[:, :, None] * f64(w_c)[:, None, :]
    v = np.einsum("krm,krt->mrt", u, picked)
    v = v + (f64(w_a).T @ f64(ment))[:, :, None]
    v = v.reshape(M, N) + f64(w_d).T @ f64(pw) + f64(b1)
    return np.maximum(v, SLOPE * v)

@@ -1,0 +1,78 @@
+import concourse.mybir as mybir
+
+BF16, F32, U16 = mybir.dt.bfloat16, mybir.dt.float32, mybir.dt.uint16
+ADD, MULT, MAX = mybir.AluOpType.add, mybir.AluOpType.mult, mybir.AluOpType.max
+IDENTITY = mybir.ActivationFunctionType.Identity
+
+P = 128
+S = 2048
+MENTIONS = 8
+PAIRS = 64
+N = MENTIONS * PAIRS
+M = 256
+HALVES = M // P
+OFFS_COLS = PAIRS // 16
+SLOPE = 0.01
+
+FLOPS = 2 * P * M * N + 2 * P * M * N + 2 * P * M * MENTIONS
+
+
+def tile_anaphoricityscorer_kernel(tc, table, ment, pw, w_a, w_b, w_c, w_d, b1, offs, out):
+    nc = tc.nc
+    with (
+        tc.tile_pool(name="held", bufs=1) as held,
+        tc.psum_pool(name="psum", bufs=1) as psum,
+    ):
+        offsets = held.tile([P, N // 16], U16, name="offsets")
+        nc.sync.dma_start(offsets[:], offs)
+        ment_sb = held.tile([P, MENTIONS], BF16, name="ment_sb")
+        nc.sync.dma_start(ment_sb[:], ment)
+        w_c_sb = held.tile([P, M], BF16, name="w_c_sb")
+        nc.sync.dma_start(w_c_sb[:], w_c)
+        w_b_sb = held.tile([P, M], BF16, name="w_b_sb")
+        nc.sync.dma_start(w_b_sb[:], w_b)
+        table_sb = held.tile([P, S], BF16, name="table_sb")
+        nc.sync.dma_start(table_sb[:], table)
+
+        pw_sb = held.tile([P, N], BF16, name="pw_sb")
+        nc.scalar.dma_start(pw_sb[:], pw)
+        w_d_sb = held.tile([P, M], BF16, name="w_d_sb")
+        nc.scalar.dma_start(w_d_sb[:], w_d)
+        w_a_sb = held.tile([P, M], BF16, name="w_a_sb")
+        nc.scalar.dma_start(w_a_sb[:], w_a)
+        bias = [held.tile([P, 1], F32, name=f"bias{h}") for h in range(HALVES)]
+        for h in range(HALVES):
+            nc.scalar.dma_start(bias[h][:], b1[h * P : (h + 1) * P, :])
+
+        u = held.tile([P, MENTIONS, M], BF16, name="u")
+        for r in range(MENTIONS):
+            nc.vector.scalar_tensor_tensor(u[:, r, :], w_c_sb[:], ment_sb[:, r : r + 1], w_b_sb[:], MULT, ADD)
+
+        ment_repeated = ment_sb[:].unsqueeze(2).to_broadcast([P, MENTIONS, PAIRS])
+        dense = []
+        for h in range(HALVES):
+            rows = slice(h * P, (h + 1) * P)
+            dense_ps = psum.tile([P, N], F32, name=f"dense_ps{h}")
+            nc.tensor.matmul(dense_ps[:], w_d_sb[:, rows], pw_sb[:], start=True, stop=False)
+            nc.tensor.matmul(
+                dense_ps[:].rearrange("p (r a) -> p r a", a=PAIRS), w_a_sb[:, rows], ment_repeated,
+                start=False, stop=True,
+            )
+            dense_sb = held.tile([P, N], F32, name=f"dense_sb{h}")
+            nc.scalar.activation(dense_sb[:], dense_ps[:], IDENTITY, bias=bias[h][:], scale=1.0)
+            dense.append(dense_sb)
+
+        for h in range(HALVES):
+            picked_ps = psum.tile([P, N], F32, name=f"picked_ps{h}")
+            for r in range(MENTIONS):
+                nc.tensor.matmul(
+                    picked_ps[:, r * PAIRS : (r + 1) * PAIRS],
+                    u[:, r, h * P : (h + 1) * P],
+                    table_sb[:].indirect(offsets[:, r * OFFS_COLS : (r + 1) * OFFS_COLS]),
+                    start=True, stop=True,
+                )
+            v = held.tile([P, N], F32, name=f"v{h}")
+            nc.vector.tensor_tensor(v[:], picked_ps[:], dense[h][:], ADD)
+            result = held.tile([P, N], F32, name=f"result{h}")
+            nc.vector.scalar_tensor_tensor(result[:], v[:], SLOPE, v[:], MULT, MAX)
+            nc.sync.dma_start(out[h * P : (h + 1) * P, :], result[:])

@@ -11,6 +11,8 @@ PAIRS = 64
 N = MENTIONS * PAIRS
 M = 256
 HALVES = M // P
+GROUP = 4
+GROUPS = MENTIONS // GROUP
 OFFS_COLS = PAIRS // 16
 SLOPE = 0.01
 
@@ -62,17 +64,20 @@ def tile_anaphoricityscorer_kernel(tc, table, ment, pw, w_a, w_b, w_c, w_d, b1, 
             nc.scalar.activation(dense_sb[:], dense_ps[:], IDENTITY, bias=bias[h][:], scale=1.0)
             dense.append(dense_sb)
 
-        for h in range(HALVES):
-            picked_ps = psum.tile([P, N], F32, name=f"picked_ps{h}")
-            for r in range(MENTIONS):
-                nc.tensor.matmul(
-                    picked_ps[:, r * PAIRS : (r + 1) * PAIRS],
-                    u[:, r, h * P : (h + 1) * P],
-                    table_sb[:].indirect(offsets[:, r * OFFS_COLS : (r + 1) * OFFS_COLS]),
-                    start=True, stop=True,
-                )
-            v = held.tile([P, N], F32, name=f"v{h}")
-            nc.vector.tensor_tensor(v[:], picked_ps[:], dense[h][:], ADD)
-            result = held.tile([P, N], F32, name=f"result{h}")
-            nc.vector.scalar_tensor_tensor(result[:], v[:], SLOPE, v[:], MULT, MAX)
-            nc.sync.dma_start(out[h * P : (h + 1) * P, :], result[:])
+        for g in range(GROUPS):
+            cols = slice(g * GROUP * PAIRS, (g + 1) * GROUP * PAIRS)
+            for h in range(HALVES):
+                picked_ps = psum.tile([P, GROUP * PAIRS], F32, name=f"picked_ps{g}{h}")
+                for i in range(GROUP):
+                    r = g * GROUP + i
+                    nc.tensor.matmul(
+                        picked_ps[:, i * PAIRS : (i + 1) * PAIRS],
+                        u[:, r, h * P : (h + 1) * P],
+                        table_sb[:].indirect(offsets[:, r * OFFS_COLS : (r + 1) * OFFS_COLS]),
+                        start=True, stop=True,
+                    )
+                v = held.tile([P, GROUP * PAIRS], F32, name=f"v{g}{h}")
+                nc.vector.tensor_tensor(v[:], picked_ps[:], dense[h][:, cols], ADD)
+                result = held.tile([P, GROUP * PAIRS], F32, name=f"result{g}{h}")
+                nc.vector.scalar_tensor_tensor(result[:], v[:], SLOPE, v[:], MULT, MAX)
+                nc.sync.dma_start(out[h * P : (h + 1) * P, cols], result[:])

@@ -15,6 +15,7 @@ GROUP = 4
 GROUPS = MENTIONS // GROUP
 OFFS_COLS = PAIRS // 16
 SLOPE = 0.01
+WARMUP = 20
 
 FLOPS = 2 * P * M * N + 2 * P * M * N + 2 * P * M * MENTIONS
 
@@ -25,6 +26,12 @@ def tile_anaphoricityscorer_kernel(tc, table, ment, pw, w_a, w_b, w_c, w_d, b1, 
         tc.tile_pool(name="held", bufs=1) as held,
         tc.psum_pool(name="psum", bufs=1) as psum,
     ):
+        warm_sb = held.tile([P, P], BF16, name="warm_sb")
+        nc.gpsimd.memset(warm_sb[:], 0.0)
+        warm_ps = psum.tile([P, P], F32, name="warm_ps")
+        for i in range(WARMUP):
+            nc.tensor.matmul(warm_ps[:], warm_sb[:], warm_sb[:], start=True, stop=True)
+
         offsets = held.tile([P, N // 16], U16, name="offsets")
         nc.sync.dma_start(offsets[:], offs)
         ment_sb = held.tile([P, MENTIONS], BF16, name="ment_sb")

@@ -15,7 +15,6 @@ GROUP = 4
 GROUPS = MENTIONS // GROUP
 OFFS_COLS = PAIRS // 16
 SLOPE = 0.01
-WARMUP = 20
 
 FLOPS = 2 * P * M * N + 2 * P * M * N + 2 * P * M * MENTIONS
 
@@ -26,32 +25,27 @@ def tile_anaphoricityscorer_kernel(tc, table, ment, pw, w_a, w_b, w_c, w_d, b1, 
         tc.tile_pool(name="held", bufs=1) as held,
         tc.psum_pool(name="psum", bufs=1) as psum,
     ):
-        warm_sb = held.tile([P, P], BF16, name="warm_sb")
-        nc.gpsimd.memset(warm_sb[:], 0.0)
-        warm_ps = psum.tile([P, P], F32, name="warm_ps")
-        for i in range(WARMUP):
-            nc.tensor.matmul(warm_ps[:], warm_sb[:], warm_sb[:], start=True, stop=True)
-
-        offsets = held.tile([P, N // 16], U16, name="offsets")
-        nc.sync.dma_start(offsets[:], offs)
-        ment_sb = held.tile([P, MENTIONS], BF16, name="ment_sb")
-        nc.sync.dma_start(ment_sb[:], ment)
         w_c_sb = held.tile([P, M], BF16, name="w_c_sb")
         nc.sync.dma_start(w_c_sb[:], w_c)
-        w_b_sb = held.tile([P, M], BF16, name="w_b_sb")
-        nc.sync.dma_start(w_b_sb[:], w_b)
+        ment_sb = held.tile([P, MENTIONS], BF16, name="ment_sb")
+        nc.sync.dma_start(ment_sb[:], ment)
+        offsets = held.tile([P, N // 16], U16, name="offsets")
+        nc.sync.dma_start(offsets[:], offs)
         table_sb = held.tile([P, S], BF16, name="table_sb")
         nc.sync.dma_start(table_sb[:], table)
 
+        w_b_sb = held.tile([P, M], BF16, name="w_b_sb")
+        nc.scalar.dma_start(w_b_sb[:], w_b)
         pw_sb = held.tile([P, N], BF16, name="pw_sb")
         nc.scalar.dma_start(pw_sb[:], pw)
         w_d_sb = held.tile([P, M], BF16, name="w_d_sb")
         nc.scalar.dma_start(w_d_sb[:], w_d)
         w_a_sb = held.tile([P, M], BF16, name="w_a_sb")
         nc.scalar.dma_start(w_a_sb[:], w_a)
+
         bias = [held.tile([P, 1], F32, name=f"bias{h}") for h in range(HALVES)]
         for h in range(HALVES):
-            nc.scalar.dma_start(bias[h][:], b1[h * P : (h + 1) * P, :])
+            nc.gpsimd.dma_start(bias[h][:], b1[h * P : (h + 1) * P, :])
 
         u = held.tile([P, MENTIONS, M], BF16, name="u")
         for r in range(MENTIONS):

@@ -2,7 +2,7 @@ import concourse.mybir as mybir
 
 BF16, F32, U16 = mybir.dt.bfloat16, mybir.dt.float32, mybir.dt.uint16
 ADD, MULT, MAX = mybir.AluOpType.add, mybir.AluOpType.mult, mybir.AluOpType.max
-IDENTITY = mybir.ActivationFunctionType.Identity
+COPY = mybir.ActivationFunctionType.Copy
 
 P = 128
 S = 2048
@@ -45,7 +45,11 @@ def tile_anaphoricityscorer_kernel(tc, table, ment, pw, w_a, w_b, w_c, w_d, b1, 
 
         bias = [held.tile([P, 1], F32, name=f"bias{h}") for h in range(HALVES)]
         for h in range(HALVES):
-            nc.gpsimd.dma_start(bias[h][:], b1[h * P : (h + 1) * P, :])
+            nc.sync.dma_start(bias[h][:], b1[h * P : (h + 1) * P, :])
+
+        scratch = held.tile([P, 1], F32, name="scratch")
+        nc.vector.memset(scratch[:], 0.0)
+        nc.scalar.activation(scratch[:], scratch[:], COPY)
 
         u = held.tile([P, MENTIONS, M], BF16, name="u")
         for r in range(MENTIONS):
@@ -62,7 +66,7 @@ def tile_anaphoricityscorer_kernel(tc, table, ment, pw, w_a, w_b, w_c, w_d, b1, 
                 start=False, stop=True,
             )
             dense_sb = held.tile([P, N], F32, name=f"dense_sb{h}")
-            nc.scalar.activation(dense_sb[:], dense_ps[:], IDENTITY, bias=bias[h][:], scale=1.0)
+            nc.scalar.activation(dense_sb[:], dense_ps[:], COPY)
             dense.append(dense_sb)
 
         for g in range(GROUPS):
@@ -78,7 +82,7 @@ def tile_anaphoricityscorer_kernel(tc, table, ment, pw, w_a, w_b, w_c, w_d, b1, 
                         start=True, stop=True,
                     )
                 v = held.tile([P, GROUP * PAIRS], F32, name=f"v{g}{h}")
-                nc.vector.tensor_tensor(v[:], picked_ps[:], dense[h][:, cols], ADD)
+                nc.vector.scalar_tensor_tensor(v[:], picked_ps[:], bias[h][:], dense[h][:, cols], ADD, ADD)
                 result = held.tile([P, GROUP * PAIRS], F32, name=f"result{g}{h}")
                 nc.vector.scalar_tensor_tensor(result[:], v[:], SLOPE, v[:], MULT, MAX)
                 nc.sync.dma_start(out[h * P : (h + 1) * P, cols], result[:])

@@ -15,6 +15,7 @@ GROUP = 4
 GROUPS = MENTIONS // GROUP
 OFFS_COLS = PAIRS // 16
 SLOPE = 0.01
+WARMUP = 16
 
 FLOPS = 2 * P * M * N + 2 * P * M * N + 2 * P * M * MENTIONS
 
@@ -25,6 +26,12 @@ def tile_anaphoricityscorer_kernel(tc, table, ment, pw, w_a, w_b, w_c, w_d, b1, 
         tc.tile_pool(name="held", bufs=1) as held,
         tc.psum_pool(name="psum", bufs=1) as psum,
     ):
+        warm_sb = held.tile([P, P], BF16, name="warm_sb")
+        nc.gpsimd.memset(warm_sb[:], 0.0)
+        warm_ps = psum.tile([P, P], F32, name="warm_ps")
+        for i in range(WARMUP):
+            nc.tensor.matmul(warm_ps[:], warm_sb[:], warm_sb[:], start=True, stop=True)
+
         w_c_sb = held.tile([P, M], BF16, name="w_c_sb")
         nc.sync.dma_start(w_c_sb[:], w_c)
         ment_sb = held.tile([P, MENTIONS], BF16, name="ment_sb")
@@ -69,8 +76,13 @@ def tile_anaphoricityscorer_kernel(tc, table, ment, pw, w_a, w_b, w_c, w_d, b1, 
             nc.scalar.activation(dense_sb[:], dense_ps[:], COPY)
             dense.append(dense_sb)
 
+        def leaky_relu_and_store(v, g, h):
+            result = held.tile([P, GROUP * PAIRS], F32, name=f"result{g}{h}")
+            nc.vector.scalar_tensor_tensor(result[:], v[:], SLOPE, v[:], MULT, MAX)
+            nc.sync.dma_start(out[h * P : (h + 1) * P, g * GROUP * PAIRS : (g + 1) * GROUP * PAIRS], result[:])
+
+        summed = []
         for g in range(GROUPS):
-            cols = slice(g * GROUP * PAIRS, (g + 1) * GROUP * PAIRS)
             for h in range(HALVES):
                 picked_ps = psum.tile([P, GROUP * PAIRS], F32, name=f"picked_ps{g}{h}")
                 for i in range(GROUP):
@@ -82,7 +94,10 @@ def tile_anaphoricityscorer_kernel(tc, table, ment, pw, w_a, w_b, w_c, w_d, b1, 
                         start=True, stop=True,
                     )
                 v = held.tile([P, GROUP * PAIRS], F32, name=f"v{g}{h}")
-                nc.vector.scalar_tensor_tensor(v[:], picked_ps[:], bias[h][:], dense[h][:, cols], ADD, ADD)
-                result = held.tile([P, GROUP * PAIRS], F32, name=f"result{g}{h}")
-                nc.vector.scalar_tensor_tensor(result[:], v[:], SLOPE, v[:], MULT, MAX)
-                nc.sync.dma_start(out[h * P : (h + 1) * P, cols], result[:])
+                nc.vector.scalar_tensor_tensor(
+                    v[:], picked_ps[:], bias[h][:], dense[h][:, g * GROUP * PAIRS : (g + 1) * GROUP * PAIRS], ADD, ADD
+                )
+                if summed:
+                    leaky_relu_and_store(*summed[-1])
+                summed.append((v, g, h))
+        leaky_relu_and_store(*summed[-1])

@@ -32,17 +32,17 @@ def tile_anaphoricityscorer_kernel(tc, table, ment, pw, w_a, w_b, w_c, w_d, b1, 
         for i in range(WARMUP):
             nc.tensor.matmul(warm_ps[:], warm_sb[:], warm_sb[:], start=True, stop=True)
 
-        w_c_sb = held.tile([P, M], BF16, name="w_c_sb")
-        nc.sync.dma_start(w_c_sb[:], w_c)
         ment_sb = held.tile([P, MENTIONS], BF16, name="ment_sb")
         nc.sync.dma_start(ment_sb[:], ment)
         offsets = held.tile([P, N // 16], U16, name="offsets")
         nc.sync.dma_start(offsets[:], offs)
+        w_c_sb = held.tile([P, M], BF16, name="w_c_sb")
+        nc.sync.dma_start(w_c_sb[:], w_c)
+        w_b_sb = held.tile([P, M], BF16, name="w_b_sb")
+        nc.sync.dma_start(w_b_sb[:], w_b)
         table_sb = held.tile([P, S], BF16, name="table_sb")
         nc.sync.dma_start(table_sb[:], table)
 
-        w_b_sb = held.tile([P, M], BF16, name="w_b_sb")
-        nc.scalar.dma_start(w_b_sb[:], w_b)
         pw_sb = held.tile([P, N], BF16, name="pw_sb")
         nc.scalar.dma_start(pw_sb[:], pw)
         w_d_sb = held.tile([P, M], BF16, name="w_d_sb")

@@ -76,10 +76,14 @@ def tile_anaphoricityscorer_kernel(tc, table, ment, pw, w_a, w_b, w_c, w_d, b1, 
             nc.scalar.activation(dense_sb[:], dense_ps[:], COPY)
             dense.append(dense_sb)
 
-        def leaky_relu_and_store(v, g, h):
+        def leaky_relu_and_store(v, g, h, parts):
             result = held.tile([P, GROUP * PAIRS], F32, name=f"result{g}{h}")
-            nc.vector.scalar_tensor_tensor(result[:], v[:], SLOPE, v[:], MULT, MAX)
-            nc.sync.dma_start(out[h * P : (h + 1) * P, g * GROUP * PAIRS : (g + 1) * GROUP * PAIRS], result[:])
+            width = GROUP * PAIRS // parts
+            for i in range(parts):
+                cols = slice(i * width, (i + 1) * width)
+                nc.vector.scalar_tensor_tensor(result[:, cols], v[:, cols], SLOPE, v[:, cols], MULT, MAX)
+                first = g * GROUP * PAIRS + i * width
+                nc.sync.dma_start(out[h * P : (h + 1) * P, first : first + width], result[:, cols])
 
         summed = []
         for g in range(GROUPS):
@@ -98,6 +102,6 @@ def tile_anaphoricityscorer_kernel(tc, table, ment, pw, w_a, w_b, w_c, w_d, b1, 
                     v[:], picked_ps[:], bias[h][:], dense[h][:, g * GROUP * PAIRS : (g + 1) * GROUP * PAIRS], ADD, ADD
                 )
                 if summed:
-                    leaky_relu_and_store(*summed[-1])
+                    leaky_relu_and_store(*summed[-1], parts=1)
                 summed.append((v, g, h))
-        leaky_relu_and_store(*summed[-1])
+        leaky_relu_and_store(*summed[-1], parts=2)

@@ -2,7 +2,7 @@ import concourse.mybir as mybir
 
 BF16, F32, U16 = mybir.dt.bfloat16, mybir.dt.float32, mybir.dt.uint16
 ADD, MULT, MAX = mybir.AluOpType.add, mybir.AluOpType.mult, mybir.AluOpType.max
-COPY = mybir.ActivationFunctionType.Copy
+COPY, IDENTITY = mybir.ActivationFunctionType.Copy, mybir.ActivationFunctionType.Identity
 
 P = 128
 S = 2048
@@ -62,19 +62,21 @@ def tile_anaphoricityscorer_kernel(tc, table, ment, pw, w_a, w_b, w_c, w_d, b1, 
         for r in range(MENTIONS):
             nc.vector.scalar_tensor_tensor(u[:, r, :], w_c_sb[:], ment_sb[:, r : r + 1], w_b_sb[:], MULT, ADD)
 
-        ment_repeated = ment_sb[:].unsqueeze(2).to_broadcast([P, MENTIONS, PAIRS])
-        dense = []
+        own_ps = psum.tile([P, HALVES, MENTIONS], F32, name="own_ps")
         for h in range(HALVES):
-            rows = slice(h * P, (h + 1) * P)
-            dense_ps = psum.tile([P, N], F32, name=f"dense_ps{h}")
-            nc.tensor.matmul(dense_ps[:], w_d_sb[:, rows], pw_sb[:], start=True, stop=False)
-            nc.tensor.matmul(
-                dense_ps[:].rearrange("p (r a) -> p r a", a=PAIRS), w_a_sb[:, rows], ment_repeated,
-                start=False, stop=True,
-            )
-            dense_sb = held.tile([P, N], F32, name=f"dense_sb{h}")
-            nc.scalar.activation(dense_sb[:], dense_ps[:], COPY)
-            dense.append(dense_sb)
+            nc.tensor.matmul(own_ps[:, h, :], w_a_sb[:, h * P : (h + 1) * P], ment_sb[:], start=True, stop=True)
+        own = held.tile([P, HALVES, MENTIONS], F32, name="own")
+        nc.scalar.activation(own[:], own_ps[:], COPY)
+
+        dense_ps = [psum.tile([P, N], F32, name=f"dense_ps{h}") for h in range(HALVES)]
+        dense = [held.tile([P, N], F32, name=f"dense_sb{h}") for h in range(HALVES)]
+        for h in range(HALVES):
+            nc.tensor.matmul(dense_ps[h][:], w_d_sb[:, h * P : (h + 1) * P], pw_sb[:], start=True, stop=True)
+        for g in range(GROUPS):
+            for h in range(HALVES):
+                for r in range(g * GROUP, (g + 1) * GROUP):
+                    cols = slice(r * PAIRS, (r + 1) * PAIRS)
+                    nc.scalar.activation(dense[h][:, cols], dense_ps[h][:, cols], IDENTITY, bias=own[:, h, r : r + 1])
 
         def leaky_relu_and_store(v, g, h, parts):
             result = held.tile([P, GROUP * PAIRS], F32, name=f"result{g}{h}")

@@ -34,12 +34,12 @@ def tile_anaphoricityscorer_kernel(tc, table, ment, pw, w_a, w_b, w_c, w_d, b1, 
 
         ment_sb = held.tile([P, MENTIONS], BF16, name="ment_sb")
         nc.sync.dma_start(ment_sb[:], ment)
-        offsets = held.tile([P, N // 16], U16, name="offsets")
-        nc.sync.dma_start(offsets[:], offs)
         w_c_sb = held.tile([P, M], BF16, name="w_c_sb")
         nc.sync.dma_start(w_c_sb[:], w_c)
         w_b_sb = held.tile([P, M], BF16, name="w_b_sb")
         nc.sync.dma_start(w_b_sb[:], w_b)
+        offsets = held.tile([P, N // 16], U16, name="offsets")
+        nc.sync.dma_start(offsets[:], offs)
         table_sb = held.tile([P, S], BF16, name="table_sb")
         nc.sync.dma_start(table_sb[:], table)
 
@@ -50,9 +50,8 @@ def tile_anaphoricityscorer_kernel(tc, table, ment, pw, w_a, w_b, w_c, w_d, b1, 
         w_a_sb = held.tile([P, M], BF16, name="w_a_sb")
         nc.scalar.dma_start(w_a_sb[:], w_a)
 
-        bias = [held.tile([P, 1], F32, name=f"bias{h}") for h in range(HALVES)]
-        for h in range(HALVES):
-            nc.sync.dma_start(bias[h][:], b1[h * P : (h + 1) * P, :])
+        bias = held.tile([P, HALVES], F32, name="bias")
+        nc.sync.dma_start(bias[:], b1.rearrange("(h p) o -> p (h o)", p=P))
 
         scratch = held.tile([P, 1], F32, name="scratch")
         nc.vector.memset(scratch[:], 0.0)
@@ -101,7 +100,7 @@ def tile_anaphoricityscorer_kernel(tc, table, ment, pw, w_a, w_b, w_c, w_d, b1, 
                     )
                 v = held.tile([P, GROUP * PAIRS], F32, name=f"v{g}{h}")
                 nc.vector.scalar_tensor_tensor(
-                    v[:], picked_ps[:], bias[h][:], dense[h][:, g * GROUP * PAIRS : (g + 1) * GROUP * PAIRS], ADD, ADD
+                    v[:], picked_ps[:], bias[:, h : h + 1], dense[h][:, g * GROUP * PAIRS : (g + 1) * GROUP * PAIRS], ADD, ADD
                 )
                 if summed:
                     leaky_relu_and_store(*summed[-1], parts=1)

@@ -38,17 +38,16 @@ def tile_anaphoricityscorer_kernel(tc, table, ment, pw, w_a, w_b, w_c, w_d, b1, 
         nc.sync.dma_start(w_c_sb[:], w_c)
         w_b_sb = held.tile([P, M], BF16, name="w_b_sb")
         nc.sync.dma_start(w_b_sb[:], w_b)
+        pw_sb = held.tile([P, N], BF16, name="pw_sb")
+        nc.sync.dma_start(pw_sb[:], pw)
+        w_d_sb = held.tile([P, M], BF16, name="w_d_sb")
+        nc.sync.dma_start(w_d_sb[:], w_d)
+        w_a_sb = held.tile([P, M], BF16, name="w_a_sb")
+        nc.sync.dma_start(w_a_sb[:], w_a)
         offsets = held.tile([P, N // 16], U16, name="offsets")
         nc.sync.dma_start(offsets[:], offs)
         table_sb = held.tile([P, S], BF16, name="table_sb")
         nc.sync.dma_start(table_sb[:], table)
-
-        pw_sb = held.tile([P, N], BF16, name="pw_sb")
-        nc.scalar.dma_start(pw_sb[:], pw)
-        w_d_sb = held.tile([P, M], BF16, name="w_d_sb")
-        nc.scalar.dma_start(w_d_sb[:], w_d)
-        w_a_sb = held.tile([P, M], BF16, name="w_a_sb")
-        nc.scalar.dma_start(w_a_sb[:], w_a)
 
         bias = held.tile([P, HALVES], F32, name="bias")
         nc.sync.dma_start(bias[:], b1.rearrange("(h p) o -> p (h o)", p=P))

import concourse.mybir as mybir

BF16, F32, U16 = mybir.dt.bfloat16, mybir.dt.float32, mybir.dt.uint16
ADD, MULT, MAX = mybir.AluOpType.add, mybir.AluOpType.mult, mybir.AluOpType.max
COPY, IDENTITY = mybir.ActivationFunctionType.Copy, mybir.ActivationFunctionType.Identity

P = 128
S = 2048
MENTIONS = 8
PAIRS = 64
N = MENTIONS * PAIRS
M = 256
HALVES = M // P
GROUP = 4
GROUPS = MENTIONS // GROUP
OFFS_COLS = PAIRS // 16
SLOPE = 0.01
WARMUP = 16

FLOPS = 2 * P * M * N + 2 * P * M * N + 2 * P * M * MENTIONS


def tile_anaphoricityscorer_kernel(tc, table, ment, pw, w_a, w_b, w_c, w_d, b1, offs, out):
    nc = tc.nc
    with (
        tc.tile_pool(name="held", bufs=1) as held,
        tc.psum_pool(name="psum", bufs=1) as psum,
    ):
        warm_sb = held.tile([P, P], BF16, name="warm_sb")
        nc.gpsimd.memset(warm_sb[:], 0.0)
        warm_ps = psum.tile([P, P], F32, name="warm_ps")
        for i in range(WARMUP):
            nc.tensor.matmul(warm_ps[:], warm_sb[:], warm_sb[:], start=True, stop=True)

        ment_sb = held.tile([P, MENTIONS], BF16, name="ment_sb")
        nc.sync.dma_start(ment_sb[:], ment)
        w_c_sb = held.tile([P, M], BF16, name="w_c_sb")
        nc.sync.dma_start(w_c_sb[:], w_c)
        w_b_sb = held.tile([P, M], BF16, name="w_b_sb")
        nc.sync.dma_start(w_b_sb[:], w_b)
        pw_sb = held.tile([P, N], BF16, name="pw_sb")
        nc.sync.dma_start(pw_sb[:], pw)
        w_d_sb = held.tile([P, M], BF16, name="w_d_sb")
        nc.sync.dma_start(w_d_sb[:], w_d)
        w_a_sb = held.tile([P, M], BF16, name="w_a_sb")
        nc.sync.dma_start(w_a_sb[:], w_a)
        offsets = held.tile([P, N // 16], U16, name="offsets")
        nc.sync.dma_start(offsets[:], offs)
        table_sb = held.tile([P, S], BF16, name="table_sb")
        nc.sync.dma_start(table_sb[:], table)

        bias = held.tile([P, HALVES], F32, name="bias")
        nc.sync.dma_start(bias[:], b1.rearrange("(h p) o -> p (h o)", p=P))

        scratch = held.tile([P, 1], F32, name="scratch")
        nc.vector.memset(scratch[:], 0.0)
        nc.scalar.activation(scratch[:], scratch[:], COPY)

        u = held.tile([P, MENTIONS, M], BF16, name="u")
        for r in range(MENTIONS):
            nc.vector.scalar_tensor_tensor(u[:, r, :], w_c_sb[:], ment_sb[:, r : r + 1], w_b_sb[:], MULT, ADD)

        own_ps = psum.tile([P, HALVES, MENTIONS], F32, name="own_ps")
        for h in range(HALVES):
            nc.tensor.matmul(own_ps[:, h, :], w_a_sb[:, h * P : (h + 1) * P], ment_sb[:], start=True, stop=True)
        own = held.tile([P, HALVES, MENTIONS], F32, name="own")
        nc.scalar.activation(own[:], own_ps[:], COPY)

        dense_ps = [psum.tile([P, N], F32, name=f"dense_ps{h}") for h in range(HALVES)]
        dense = [held.tile([P, N], F32, name=f"dense_sb{h}") for h in range(HALVES)]
        for h in range(HALVES):
            nc.tensor.matmul(dense_ps[h][:], w_d_sb[:, h * P : (h + 1) * P], pw_sb[:], start=True, stop=True)
        for g in range(GROUPS):
            for h in range(HALVES):
                for r in range(g * GROUP, (g + 1) * GROUP):
                    cols = slice(r * PAIRS, (r + 1) * PAIRS)
                    nc.scalar.activation(dense[h][:, cols], dense_ps[h][:, cols], IDENTITY, bias=own[:, h, r : r + 1])

        def leaky_relu_and_store(v, g, h, parts):
            result = held.tile([P, GROUP * PAIRS], F32, name=f"result{g}{h}")
            width = GROUP * PAIRS // parts
            for i in range(parts):
                cols = slice(i * width, (i + 1) * width)
                nc.vector.scalar_tensor_tensor(result[:, cols], v[:, cols], SLOPE, v[:, cols], MULT, MAX)
                first = g * GROUP * PAIRS + i * width
                nc.sync.dma_start(out[h * P : (h + 1) * P, first : first + width], result[:, cols])

        summed = []
        for g in range(GROUPS):
            for h in range(HALVES):
                picked_ps = psum.tile([P, GROUP * PAIRS], F32, name=f"picked_ps{g}{h}")
                for i in range(GROUP):
                    r = g * GROUP + i
                    nc.tensor.matmul(
                        picked_ps[:, i * PAIRS : (i + 1) * PAIRS],
                        u[:, r, h * P : (h + 1) * P],
                        table_sb[:].indirect(offsets[:, r * OFFS_COLS : (r + 1) * OFFS_COLS]),
                        start=True, stop=True,
                    )
                v = held.tile([P, GROUP * PAIRS], F32, name=f"v{g}{h}")
                nc.vector.scalar_tensor_tensor(
                    v[:], picked_ps[:], bias[:, h : h + 1], dense[h][:, g * GROUP * PAIRS : (g + 1) * GROUP * PAIRS], ADD, ADD
                )
                if summed:
                    leaky_relu_and_store(*summed[-1], parts=1)
                summed.append((v, g, h))
        leaky_relu_and_store(*summed[-1], parts=2)
